import numpy as np
import ml_dtypes


def mxq(x, axis, fmt="e4m3"):
    dtype, down = {"e4m3": (ml_dtypes.float8_e4m3fn, 7), "e5m2": (ml_dtypes.float8_e5m2, 14)}[fmt]
    v = np.moveaxis(np.asarray(x, np.float32).astype(ml_dtypes.bfloat16).astype(np.float64), axis, -1)
    blocks = v.reshape(v.shape[:-1] + (-1, 32))
    amax = np.abs(blocks).max(-1, keepdims=True)
    byte = np.maximum(np.where(amax > 0, np.frexp(amax)[1] - 1 + 127, 0) - down, 1)
    scale = np.exp2(byte - 127.0)
    codes = (blocks / scale).astype(np.float32).astype(dtype).astype(np.float64)
    return np.moveaxis((codes * scale).reshape(v.shape), -1, axis)


WIDE = False


def mx_kscale(k):
    if not WIDE:
        return np.ones(k)
    levels = np.array([10, -10, 5, -5, 0])
    a = np.random.permutation(np.resize(levels, k // 512 * 4)).reshape(k // 512, 4)
    idx = np.arange(k)
    return np.exp2(a[idx // 512, idx % 128 // 32])


BF16 = ml_dtypes.bfloat16


def bf(x):
    return np.asarray(x, np.float32).astype(BF16)


def f64(x):
    return np.asarray(x).astype(np.float64)


B, L, H = 2, 1024, 1024


def setup_inputs():
    s = mx_kscale(H)
    return {"q": bf(np.random.standard_normal((B, L, H)) * 0.1 * s),
            "h_rot": bf(np.random.standard_normal((B, L, H)) * 0.2 / s)}


def reference(q, h_rot):
    h = f64(h_rot)
    pre_attn = mxq(f64(q), 2, "e4m3") @ mxq(h, 2, "e4m3").transpose(0, 2, 1)
    return mxq(pre_attn, 2, "e4m3") @ mxq(h, 1, "e4m3")

@@ -1,0 +1,188 @@
+from contextlib import ExitStack
+
+import concourse.mybir as mybir
+from concourse.masks import make_identity
+
+F32 = mybir.dt.float32
+BF16 = mybir.dt.bfloat16
+U32 = mybir.dt.uint32
+U8 = mybir.dt.uint8
+FP8X4 = mybir.dt.float8_e4m3fn_x4
+
+L = 1024
+H = 1024
+P = 128
+FLOPS = 8 * L * L * H
+
+LEAD = 4
+STEPS = 16
+
+
+def tile_denseattentiononehead_pb_kernel(tc, q, h_rot, out):
+    nc = tc.nc
+    with ExitStack() as ctx:
+        const = ctx.enter_context(tc.tile_pool(name="const", bufs=1))
+        inputs = ctx.enter_context(tc.tile_pool(name="inputs", bufs=1))
+        codes = ctx.enter_context(tc.tile_pool(name="codes", bufs=1))
+        stage_t = ctx.enter_context(tc.tile_pool(name="stage_t", bufs=6))
+        stage_h = ctx.enter_context(tc.tile_pool(name="stage_h", bufs=2))
+        stage_s = ctx.enter_context(tc.tile_pool(name="stage_s", bufs=3))
+        stage_o = ctx.enter_context(tc.tile_pool(name="stage_o", bufs=8))
+        psum = ctx.enter_context(tc.psum_pool(name="psum", bufs=8))
+        ctx.enter_context(tc.manual_schedule())
+
+        ident = const.tile([P, P], F32, name="ident")
+        make_identity(nc, ident[:])
+
+        dram = {
+            "q": q.rearrange("b (a p t) w -> b a p t w", a=2, p=P, t=4),
+            "h": h_rot.rearrange("b (a p t) w -> b a p t w", a=2, p=P, t=4),
+        }
+        out_view = out.rearrange("b (a p t) n -> b a t p n", a=2, p=P, t=4)
+        rows = {}
+        staged = {}
+        mx = {}
+
+        def load(x, b, half, pieces):
+            rows[(x, b, half)] = inputs.tile([P, 4 * H], BF16, name="in_%s%d%d" % (x, b, half), align_bytes=64)
+            dst = rows[(x, b, half)]
+            if pieces == 4:
+                for t in range(4):
+                    nc.sync.dma_start(out=dst[:, t * H : (t + 1) * H], in_=dram[x][b, half, :, t, :])
+            else:
+                nc.sync.dma_start(out=dst[:].rearrange("p (t w) -> p t w", t=4), in_=dram[x][b, half])
+
+        def quantise(key, width):
+            words = codes.tile([P, width], U32, name="c_%s_%s_%d_%d" % key, align_bytes=64)
+            scales = codes.tile([P, width], U8, name="s_%s_%s_%d_%d" % key, align_bytes=64)
+            nc.vector.quantize_mx(out=words[:].bitcast(FP8X4), scales=scales[:], in_=staged[key][:])
+            mx[key] = (words, scales)
+
+        def transpose_rows(x, b, rt, engine):
+            words = rows[(x, b, rt // 4)][:].bitcast(F32)
+            bank = psum.tile([P, 512], F32, name="bank", tag="bank")
+            for wt in range(4):
+                col = 512 * (rt % 4) + P * wt
+                nc.tensor.transpose(bank[:, P * wt : P * (wt + 1)], words[:, col : col + P], ident[:])
+            grouped = stage_t.tile([P, 1024], BF16, name="g_t", tag="g_t", align_bytes=64)
+            engine(
+                out=grouped[:].bitcast(F32).rearrange("p (g r u) -> p g r u", g=2, r=P, u=2),
+                in_=bank[:].rearrange("p (g u r) -> p g r u", g=2, u=2, r=P),
+            )
+            staged[("t", x, b, rt)] = grouped
+
+        def prepare(x, b, half, share):
+            for t in range(4):
+                transpose_rows(x, b, 4 * half + t, nc.vector.tensor_copy if (share and t == 0) else nc.scalar.copy)
+            for t in range(4):
+                quantise(("t", x, b, 4 * half + t), 256)
+
+        def values(b, g2, nh):
+            src = rows[("h", b, g2)][:].rearrange("p (t n) -> p t n", t=4)[:, :, 512 * nh : 512 * (nh + 1)]
+            grouped = stage_h.tile([P, 2048], BF16, name="g_h", tag="g_h", align_bytes=64)
+            nc.vector.tensor_copy(
+                out=grouped[:].rearrange("p (c i t) -> p c t i", c=P, i=4, t=4),
+                in_=src.rearrange("p t (c i) -> p c t i", i=4),
+            )
+            staged[("k", "h", 2 * b + g2, nh)] = grouped
+
+        def scores(s):
+            b, it = divmod(s, 8)
+            q_words, q_scales = mx[("t", "q", b, it)]
+            grouped = stage_s.tile([P, 1024], BF16, name="g_s", tag="g_s", align_bytes=64)
+            for g2 in range(2):
+                bank = psum.tile([P, 512], F32, name="bank", tag="bank")
+                for t in range(4):
+                    h_words, h_scales = mx[("t", "h", b, 4 * g2 + t)]
+                    for g in range(2):
+                        cols = slice(P * g, P * (g + 1))
+                        nc.tensor.matmul_mx(
+                            out=bank[:, P * t : P * (t + 1)],
+                            lhsT=h_words[:, cols].bitcast(FP8X4),
+                            lhsT_scale=h_scales[:, cols],
+                            rhs=q_words[:, cols].bitcast(FP8X4),
+                            rhs_scale=q_scales[:, cols],
+                            start=(g == 0),
+                            stop=(g == 1),
+                        )
+                nc.scalar.copy(
+                    out=grouped[:, 512 * g2 : 512 * (g2 + 1)].rearrange("p (i t) -> p i t", t=4),
+                    in_=bank[:].rearrange("p (t i) -> p i t", t=4),
+                )
+            staged[("s", "s", b, it)] = grouped
+
+        def outputs(s):
+            b, it = divmod(s, 8)
+            s_words, s_scales = mx[("s", "s", b, it)]
+            for nh in range(2):
+                bank = psum.tile([P, 512], F32, name="bank", tag="bank")
+                for g2 in range(2):
+                    k_words, k_scales = mx[("k", "h", 2 * b + g2, nh)]
+                    cols = slice(P * g2, P * (g2 + 1))
+                    nc.tensor.matmul_mx(
+                        out=bank[:],
+                        lhsT=s_words[:, cols].bitcast(FP8X4),
+                        lhsT_scale=s_scales[:, cols],
+                        rhs=k_words[:].bitcast(FP8X4),
+                        rhs_scale=k_scales[:],
+                        start=(g2 == 0),
+                        stop=(g2 == 1),
+                    )
+                result = stage_o.tile([P, 512], F32, name="o_sb", tag="o_sb")
+                if nh == 0:
+                    nc.scalar.copy(out=result[:], in_=bank[:])
+                else:
+                    nc.vector.tensor_copy(out=result[:], in_=bank[:])
+                nc.sync.dma_start(out=out_view[b, it // 4, it % 4, :, 512 * nh : 512 * (nh + 1)], in_=result[:])
+
+        load("h", 0, 0, 4)
+        load("h", 0, 1, 4)
+        load("q", 0, 0, 4)
+        load("q", 0, 1, 1)
+        load("h", 1, 0, 1)
+        load("h", 1, 1, 1)
+        load("q", 1, 0, 1)
+        load("q", 1, 1, 1)
+
+        def values_unit(b, g2, nh):
+            values(b, g2, nh)
+            quantise(("k", "h", 2 * b + g2, nh), 512)
+
+        def step(s):
+            if 1 <= s <= STEPS:
+                quantise(("s", "s", (s - 1) // 8, (s - 1) % 8), 256)
+            if s < STEPS:
+                scores(s)
+            if s >= LEAD:
+                outputs(s - LEAD)
+
+        prepare("h", 0, 0, False)
+        values(0, 0, 0)
+        prepare("h", 0, 1, False)
+        quantise(("k", "h", 0, 0), 512)
+        prepare("q", 0, 0, False)
+        step(0)
+        values_unit(0, 0, 1)
+        step(1)
+        prepare("q", 0, 1, False)
+        values_unit(0, 1, 0)
+        step(2)
+        values_unit(0, 1, 1)
+        step(3)
+        prepare("h", 1, 0, True)
+        step(4)
+        values_unit(1, 0, 0)
+        step(5)
+        prepare("h", 1, 1, True)
+        step(6)
+        prepare("q", 1, 0, True)
+        step(7)
+        values_unit(1, 0, 1)
+        step(8)
+        values_unit(1, 1, 0)
+        step(9)
+        prepare("q", 1, 1, True)
+        step(10)
+        values_unit(1, 1, 1)
+        for s in range(11, STEPS + LEAD):
+            step(s)

@@ -33,6 +33,13 @@ def tile_denseattentiononehead_pb_kernel(tc, q, h_rot, out):
 
         ident = const.tile([P, P], F32, name="ident")
         make_identity(nc, ident[:])
+        zeros = const.tile([P, 512], BF16, name="zeros")
+        nc.vector.memset(zeros[:], 0.0)
+
+        def keep_clock_up(count):
+            for k in range(count):
+                bank = psum.tile([P, 512], F32, name="bank", tag="bank")
+                nc.tensor.matmul(out=bank[:], lhsT=zeros[:, 0:P], rhs=zeros[:], start=True, stop=True)
 
         dram = {
             "q": q.rearrange("b (a p t) w -> b a p t w", a=2, p=P, t=4),
@@ -74,6 +81,8 @@ def tile_denseattentiononehead_pb_kernel(tc, q, h_rot, out):
         def prepare(x, b, half, share):
             for t in range(4):
                 transpose_rows(x, b, 4 * half + t, nc.vector.tensor_copy if (share and t == 0) else nc.scalar.copy)
+                if not share and (x, half) != ("q", 1) and t % 2 == 1:
+                    keep_clock_up(1)
             for t in range(4):
                 quantise(("t", x, b, 4 * half + t), 256)
 
@@ -156,6 +165,7 @@ def tile_denseattentiononehead_pb_kernel(tc, q, h_rot, out):
             if s >= LEAD:
                 outputs(s - LEAD)
 
+        keep_clock_up(8)
         prepare("h", 0, 0, False)
         values(0, 0, 0)
         prepare("h", 0, 1, False)

@@ -29,17 +29,9 @@ def tile_denseattentiononehead_pb_kernel(tc, q, h_rot, out):
         stage_s = ctx.enter_context(tc.tile_pool(name="stage_s", bufs=3))
         stage_o = ctx.enter_context(tc.tile_pool(name="stage_o", bufs=8))
         psum = ctx.enter_context(tc.psum_pool(name="psum", bufs=8))
-        ctx.enter_context(tc.manual_schedule())
 
         ident = const.tile([P, P], F32, name="ident")
         make_identity(nc, ident[:])
-        zeros = const.tile([P, 512], BF16, name="zeros")
-        nc.vector.memset(zeros[:], 0.0)
-
-        def keep_clock_up(count):
-            for k in range(count):
-                bank = psum.tile([P, 512], F32, name="bank", tag="bank")
-                nc.tensor.matmul(out=bank[:], lhsT=zeros[:, 0:P], rhs=zeros[:], start=True, stop=True)
 
         dram = {
             "q": q.rearrange("b (a p t) w -> b a p t w", a=2, p=P, t=4),
@@ -81,8 +73,6 @@ def tile_denseattentiononehead_pb_kernel(tc, q, h_rot, out):
         def prepare(x, b, half, share):
             for t in range(4):
                 transpose_rows(x, b, 4 * half + t, nc.vector.tensor_copy if (share and t == 0) else nc.scalar.copy)
-                if not share and (x, half) != ("q", 1) and t % 2 == 1:
-                    keep_clock_up(1)
             for t in range(4):
                 quantise(("t", x, b, 4 * half + t), 256)
 
@@ -165,7 +155,6 @@ def tile_denseattentiononehead_pb_kernel(tc, q, h_rot, out):
             if s >= LEAD:
                 outputs(s - LEAD)
 
-        keep_clock_up(8)
         prepare("h", 0, 0, False)
         values(0, 0, 0)
         prepare("h", 0, 1, False)

@@ -29,6 +29,7 @@ def tile_denseattentiononehead_pb_kernel(tc, q, h_rot, out):
         stage_s = ctx.enter_context(tc.tile_pool(name="stage_s", bufs=3))
         stage_o = ctx.enter_context(tc.tile_pool(name="stage_o", bufs=8))
         psum = ctx.enter_context(tc.psum_pool(name="psum", bufs=8))
+        ctx.enter_context(tc.manual_schedule())
 
         ident = const.tile([P, P], F32, name="ident")
         make_identity(nc, ident[:])
@@ -70,11 +71,17 @@ def tile_denseattentiononehead_pb_kernel(tc, q, h_rot, out):
             )
             staged[("t", x, b, rt)] = grouped
 
-        def prepare(x, b, half, share):
+        def transposes(x, b, half, share):
             for t in range(4):
                 transpose_rows(x, b, 4 * half + t, nc.vector.tensor_copy if (share and t == 0) else nc.scalar.copy)
+
+        def quantise_rows(x, b, half):
             for t in range(4):
                 quantise(("t", x, b, 4 * half + t), 256)
+
+        def prepare(x, b, half, share):
+            transposes(x, b, half, share)
+            quantise_rows(x, b, half)
 
         def values(b, g2, nh):
             src = rows[("h", b, g2)][:].rearrange("p (t n) -> p t n", t=4)[:, :, 512 * nh : 512 * (nh + 1)]
@@ -163,8 +170,9 @@ def tile_denseattentiononehead_pb_kernel(tc, q, h_rot, out):
         step(0)
         values_unit(0, 0, 1)
         step(1)
-        prepare("q", 0, 1, False)
+        transposes("q", 0, 1, False)
         values_unit(0, 1, 0)
+        quantise_rows("q", 0, 1)
         step(2)
         values_unit(0, 1, 1)
         step(3)

@@ -14,8 +14,9 @@ H = 1024
 P = 128
 FLOPS = 8 * L * L * H
 
-LEAD = 4
+LEAD = 6
 STEPS = 16
+VEC_FROM = 8
 
 
 def tile_denseattentiononehead_pb_kernel(tc, q, h_rot, out):
@@ -24,10 +25,11 @@ def tile_denseattentiononehead_pb_kernel(tc, q, h_rot, out):
         const = ctx.enter_context(tc.tile_pool(name="const", bufs=1))
         inputs = ctx.enter_context(tc.tile_pool(name="inputs", bufs=1))
         codes = ctx.enter_context(tc.tile_pool(name="codes", bufs=1))
-        stage_t = ctx.enter_context(tc.tile_pool(name="stage_t", bufs=6))
-        stage_h = ctx.enter_context(tc.tile_pool(name="stage_h", bufs=2))
-        stage_s = ctx.enter_context(tc.tile_pool(name="stage_s", bufs=3))
-        stage_o = ctx.enter_context(tc.tile_pool(name="stage_o", bufs=8))
+        stage_t = ctx.enter_context(tc.tile_pool(name="stage_t", bufs=12))
+        stage_q = ctx.enter_context(tc.tile_pool(name="stage_q", bufs=2))
+        stage_h = ctx.enter_context(tc.tile_pool(name="stage_h", bufs=3))
+        stage_s = ctx.enter_context(tc.tile_pool(name="stage_s", bufs=4))
+        stage_o = ctx.enter_context(tc.tile_pool(name="stage_o", bufs=16))
         psum = ctx.enter_context(tc.psum_pool(name="psum", bufs=8))
         ctx.enter_context(tc.manual_schedule())
 
@@ -40,23 +42,28 @@ def tile_denseattentiononehead_pb_kernel(tc, q, h_rot, out):
         }
         out_view = out.rearrange("b (a p t) n -> b a t p n", a=2, p=P, t=4)
         rows = {}
+        blocks = {}
+        pending = []
+        block_words = {}
+        block_scales = {}
         staged = {}
         mx = {}
 
         def load(x, b, half, pieces):
-            rows[(x, b, half)] = inputs.tile([P, 4 * H], BF16, name="in_%s%d%d" % (x, b, half), align_bytes=64)
+            if (x, b, half) not in rows:
+                rows[(x, b, half)] = inputs.tile([P, 4 * H], BF16, name="in_%s%d%d" % (x, b, half), align_bytes=64)
             dst = rows[(x, b, half)]
-            if pieces == 4:
-                for t in range(4):
-                    nc.sync.dma_start(out=dst[:, t * H : (t + 1) * H], in_=dram[x][b, half, :, t, :])
-            else:
+            if pieces is None:
                 nc.sync.dma_start(out=dst[:].rearrange("p (t w) -> p t w", t=4), in_=dram[x][b, half])
+            else:
+                for t in pieces:
+                    nc.sync.dma_start(out=dst[:, t * H : (t + 1) * H], in_=dram[x][b, half, :, t, :])
 
         def quantise(key, width):
             words = codes.tile([P, width], U32, name="c_%s_%s_%d_%d" % key, align_bytes=64)
             scales = codes.tile([P, width], U8, name="s_%s_%s_%d_%d" % key, align_bytes=64)
             nc.vector.quantize_mx(out=words[:].bitcast(FP8X4), scales=scales[:], in_=staged[key][:])
-            mx[key] = (words, scales)
+            mx[key] = (words, scales, (0, P))
 
         def transpose_rows(x, b, rt, engine):
             words = rows[(x, b, rt // 4)][:].bitcast(F32)
@@ -75,6 +82,39 @@ def tile_denseattentiononehead_pb_kernel(tc, q, h_rot, out):
             for t in range(4):
                 transpose_rows(x, b, 4 * half + t, nc.vector.tensor_copy if (share and t == 0) else nc.scalar.copy)
 
+        def load_blocks(b, half):
+            blocks[half] = inputs.tile([P, 4 * H], BF16, name="blk_q%d%d" % (b, half), align_bytes=64)
+            for g in range(2):
+                for qu in range(4):
+                    for u in range(2):
+                        k0 = 512 * g + 256 * u + 64 * qu
+                        nc.sync.dma_start(
+                            out=blocks[half][32 * qu + u : 32 * (qu + 1) : 2, 2048 * g : 2048 * (g + 1)].rearrange(
+                                "c (r w) -> c r w", w=64
+                            ),
+                            in_=q[b, 512 * half : 512 * (half + 1), k0 : k0 + 64].rearrange("(r c) w -> c r w", c=16),
+                        )
+
+        def turn_blocks(b, half, g):
+            turned = stage_q.tile([P, 2048], BF16, name="g_q", tag="g_q", align_bytes=64)
+            nc.vector.transpose(
+                out=turned[:].bitcast(F32), in_=blocks[half][:, 2048 * g : 2048 * (g + 1)].bitcast(F32)
+            )
+            staged[("b", half, g)] = turned
+
+        def quantise_blocks(b, half, g):
+            if g == 0:
+                block_words[half] = codes.tile([P, 1024], U32, name="c_b%d" % half, align_bytes=64)
+                block_scales[half] = codes.tile([P, 1024], U8, name="s_b%d" % half, align_bytes=64)
+            cols = slice(512 * g, 512 * (g + 1))
+            nc.vector.quantize_mx(
+                out=block_words[half][:, cols].bitcast(FP8X4),
+                scales=block_scales[half][:, cols],
+                in_=staged[("b", half, g)][:],
+            )
+            for t in range(4):
+                mx[("t", "q", b, 4 * half + t)] = (block_words[half], block_scales[half], (P * t, 512 + P * t))
+
         def quantise_rows(x, b, half):
             for t in range(4):
                 quantise(("t", x, b, 4 * half + t), 256)
@@ -92,22 +132,25 @@ def tile_denseattentiononehead_pb_kernel(tc, q, h_rot, out):
             )
             staged[("k", "h", 2 * b + g2, nh)] = grouped
 
-        def scores(s):
+        def scores(s, parts):
             b, it = divmod(s, 8)
-            q_words, q_scales = mx[("t", "q", b, it)]
-            grouped = stage_s.tile([P, 1024], BF16, name="g_s", tag="g_s", align_bytes=64)
-            for g2 in range(2):
+            q_words, q_scales, q_cols = mx[("t", "q", b, it)]
+            if 0 in parts:
+                staged[("s", "s", b, it)] = stage_s.tile([P, 1024], BF16, name="g_s", tag="g_s", align_bytes=64)
+            grouped = staged[("s", "s", b, it)]
+            for g2 in parts:
                 bank = psum.tile([P, 512], F32, name="bank", tag="bank")
                 for t in range(4):
-                    h_words, h_scales = mx[("t", "h", b, 4 * g2 + t)]
+                    h_words, h_scales, h_cols = mx[("t", "h", b, 4 * g2 + t)]
                     for g in range(2):
-                        cols = slice(P * g, P * (g + 1))
+                        hc = slice(h_cols[g], h_cols[g] + P)
+                        qc = slice(q_cols[g], q_cols[g] + P)
                         nc.tensor.matmul_mx(
                             out=bank[:, P * t : P * (t + 1)],
-                            lhsT=h_words[:, cols].bitcast(FP8X4),
-                            lhsT_scale=h_scales[:, cols],
-                            rhs=q_words[:, cols].bitcast(FP8X4),
-                            rhs_scale=q_scales[:, cols],
+                            lhsT=h_words[:, hc].bitcast(FP8X4),
+                            lhsT_scale=h_scales[:, hc],
+                            rhs=q_words[:, qc].bitcast(FP8X4),
+                            rhs_scale=q_scales[:, qc],
                             start=(g == 0),
                             stop=(g == 1),
                         )
@@ -115,15 +158,14 @@ def tile_denseattentiononehead_pb_kernel(tc, q, h_rot, out):
                     out=grouped[:, 512 * g2 : 512 * (g2 + 1)].rearrange("p (i t) -> p i t", t=4),
                     in_=bank[:].rearrange("p (t i) -> p i t", t=4),
                 )
-            staged[("s", "s", b, it)] = grouped
 
         def outputs(s):
             b, it = divmod(s, 8)
-            s_words, s_scales = mx[("s", "s", b, it)]
+            s_words, s_scales, s_cols = mx[("s", "s", b, it)]
             for nh in range(2):
                 bank = psum.tile([P, 512], F32, name="bank", tag="bank")
                 for g2 in range(2):
-                    k_words, k_scales = mx[("k", "h", 2 * b + g2, nh)]
+                    k_words, k_scales, k_cols = mx[("k", "h", 2 * b + g2, nh)]
                     cols = slice(P * g2, P * (g2 + 1))
                     nc.tensor.matmul_mx(
                         out=bank[:],
@@ -134,62 +176,146 @@ def tile_denseattentiononehead_pb_kernel(tc, q, h_rot, out):
                         start=(g2 == 0),
                         stop=(g2 == 1),
                     )
-                result = stage_o.tile([P, 512], F32, name="o_sb", tag="o_sb")
-                if nh == 0:
-                    nc.scalar.copy(out=result[:], in_=bank[:])
+                if s < VEC_FROM or nh == 0:
+                    drain(b, it, nh, bank, nc.scalar.copy)
                 else:
-                    nc.vector.tensor_copy(out=result[:], in_=bank[:])
-                nc.sync.dma_start(out=out_view[b, it // 4, it % 4, :, 512 * nh : 512 * (nh + 1)], in_=result[:])
+                    pending.append((b, it, nh, bank))
 
-        load("h", 0, 0, 4)
-        load("h", 0, 1, 4)
-        load("q", 0, 0, 4)
-        load("q", 0, 1, 1)
-        load("h", 1, 0, 1)
-        load("h", 1, 1, 1)
-        load("q", 1, 0, 1)
-        load("q", 1, 1, 1)
+        def drain(b, it, nh, bank, engine):
+            result = stage_o.tile([P, 512], F32, name="o_sb", tag="o_sb")
+            engine(out=result[:], in_=bank[:])
+            cols = slice(512 * nh, 512 * (nh + 1))
+            if b == 0:
+                nc.sync.dma_start(out=out_view[b, it // 4, it % 4, :, cols], in_=result[:])
+            else:
+                nc.sync.dma_start(out=out[b, P * it : P * (it + 1), cols], in_=result[:])
 
-        def values_unit(b, g2, nh):
+        load("h", 0, 0, range(4))
+        load("q", 0, 0, range(1))
+        load("h", 0, 1, range(4))
+        load("q", 0, 0, range(1, 4))
+        load("q", 0, 1, range(4))
+        load("h", 1, 0, range(4))
+        load("h", 1, 1, range(4))
+        load_blocks(1, 0)
+
+        def kv(b, g2, nh):
             values(b, g2, nh)
+
+        def kq(b, g2, nh):
             quantise(("k", "h", 2 * b + g2, nh), 512)
 
+        def tr(x, b, rt):
+            transpose_rows(x, b, rt, nc.scalar.copy)
+
+        def qz(x, b, rt):
+            quantise(("t", x, b, rt), 256)
+
+        def qs(s):
+            quantise(("s", "s", s // 8, s % 8), 256)
+
+        def flush():
+            for b, it, nh, bank in pending:
+                drain(b, it, nh, bank, nc.vector.tensor_copy)
+            pending.clear()
+
         def step(s):
-            if 1 <= s <= STEPS:
-                quantise(("s", "s", (s - 1) // 8, (s - 1) % 8), 256)
             if s < STEPS:
-                scores(s)
+                scores(s, range(2))
             if s >= LEAD:
                 outputs(s - LEAD)
 
-        prepare("h", 0, 0, False)
-        values(0, 0, 0)
-        prepare("h", 0, 1, False)
-        quantise(("k", "h", 0, 0), 512)
-        prepare("q", 0, 0, False)
-        step(0)
-        values_unit(0, 0, 1)
+        for rt in range(4):
+            tr("h", 0, rt)
+        tr("q", 0, 0)
+        for rt in range(4):
+            qz("h", 0, rt)
+        qz("q", 0, 0)
+        tr("h", 0, 4)
+        tr("h", 0, 5)
+        kv(0, 0, 0)
+        scores(0, range(1))
+        for rt in range(6, 8):
+            tr("h", 0, rt)
+        tr("q", 0, 1)
+        for rt in range(4, 8):
+            qz("h", 0, rt)
+        qz("q", 0, 1)
+        scores(0, range(1, 2))
+        kq(0, 0, 0)
+        tr("q", 0, 2)
+        tr("q", 0, 3)
+        qz("q", 0, 2)
+        qz("q", 0, 3)
         step(1)
-        transposes("q", 0, 1, False)
-        values_unit(0, 1, 0)
-        quantise_rows("q", 0, 1)
+        kv(0, 0, 1)
+        qs(0)
+        kq(0, 0, 1)
         step(2)
-        values_unit(0, 1, 1)
+        kv(0, 1, 0)
+        for rt in range(4, 8):
+            tr("q", 0, rt)
+        qs(1)
+        kq(0, 1, 0)
         step(3)
-        prepare("h", 1, 0, True)
+        for rt in range(4, 8):
+            qz("q", 0, rt)
+        kv(0, 1, 1)
+        qs(2)
+        kq(0, 1, 1)
+        for rt in range(4):
+            tr("h", 1, rt)
         step(4)
-        values_unit(1, 0, 0)
+        qs(3)
+        for rt in range(4):
+            qz("h", 1, rt)
+        for rt in range(4, 8):
+            tr("h", 1, rt)
         step(5)
-        prepare("h", 1, 1, True)
+        load_blocks(1, 1)
+        qs(4)
+        turn_blocks(1, 0, 0)
+        turn_blocks(1, 0, 1)
         step(6)
-        prepare("q", 1, 0, True)
+        qs(5)
+        quantise_blocks(1, 0, 0)
+        quantise_blocks(1, 0, 1)
+        for rt in range(4, 8):
+            qz("h", 1, rt)
         step(7)
-        values_unit(1, 0, 1)
+        qs(6)
+        kv(1, 0, 0)
         step(8)
-        values_unit(1, 1, 0)
+        qs(7)
+        kq(1, 0, 0)
+        kv(1, 1, 0)
+        flush()
         step(9)
-        prepare("q", 1, 1, True)
+        qs(8)
+        kq(1, 1, 0)
+        turn_blocks(1, 1, 0)
+        flush()
         step(10)
-        values_unit(1, 1, 1)
-        for s in range(11, STEPS + LEAD):
+        qs(9)
+        turn_blocks(1, 1, 1)
+        quantise_blocks(1, 1, 0)
+        quantise_blocks(1, 1, 1)
+        flush()
+        step(11)
+        qs(10)
+        kv(1, 0, 1)
+        flush()
+        step(12)
+        qs(11)
+        kq(1, 0, 1)
+        kv(1, 1, 1)
+        flush()
+        step(13)
+        qs(12)
+        kq(1, 1, 1)
+        flush()
+        for s in range(14, STEPS + LEAD):
             step(s)
+            if s - 1 < STEPS:
+                qs(s - 1)
+            flush()

@@ -14,9 +14,7 @@ H = 1024
 P = 128
 FLOPS = 8 * L * L * H
 
-LEAD = 6
 STEPS = 16
-VEC_FROM = 8
 
 
 def tile_denseattentiononehead_pb_kernel(tc, q, h_rot, out):
@@ -33,6 +31,8 @@ def tile_denseattentiononehead_pb_kernel(tc, q, h_rot, out):
         psum = ctx.enter_context(tc.psum_pool(name="psum", bufs=8))
         ctx.enter_context(tc.manual_schedule())
 
+        blank = const.tile([P, 512], BF16, name="blank", align_bytes=64)
+        nc.gpsimd.memset(blank[:], 0.0)
         ident = const.tile([P, P], F32, name="ident")
         make_identity(nc, ident[:])
 
@@ -159,7 +159,7 @@ def tile_denseattentiononehead_pb_kernel(tc, q, h_rot, out):
                     in_=bank[:].rearrange("p (t i) -> p i t", t=4),
                 )
 
-        def outputs(s):
+        def outputs(s, vec=()):
             b, it = divmod(s, 8)
             s_words, s_scales, s_cols = mx[("s", "s", b, it)]
             for nh in range(2):
@@ -176,28 +176,28 @@ def tile_denseattentiononehead_pb_kernel(tc, q, h_rot, out):
                         start=(g2 == 0),
                         stop=(g2 == 1),
                     )
-                if s < VEC_FROM or nh == 0:
-                    drain(b, it, nh, bank, nc.scalar.copy)
-                else:
+                if nh in vec:
                     pending.append((b, it, nh, bank))
+                else:
+                    drain(b, it, nh, bank, nc.scalar.copy)
 
         def drain(b, it, nh, bank, engine):
             result = stage_o.tile([P, 512], F32, name="o_sb", tag="o_sb")
             engine(out=result[:], in_=bank[:])
             cols = slice(512 * nh, 512 * (nh + 1))
-            if b == 0:
+            if b == 0 or it < 4:
                 nc.sync.dma_start(out=out_view[b, it // 4, it % 4, :, cols], in_=result[:])
             else:
                 nc.sync.dma_start(out=out[b, P * it : P * (it + 1), cols], in_=result[:])
 
         load("h", 0, 0, range(4))
-        load("q", 0, 0, range(1))
         load("h", 0, 1, range(4))
-        load("q", 0, 0, range(1, 4))
+        load("q", 0, 0, range(4))
         load("q", 0, 1, range(4))
-        load("h", 1, 0, range(4))
-        load("h", 1, 1, range(4))
-        load_blocks(1, 0)
+        load("h", 1, 0, None)
+        load("h", 1, 1, None)
+        load("q", 1, 0, None)
+        load_blocks(1, 1)
 
         def kv(b, g2, nh):
             values(b, g2, nh)
@@ -207,6 +207,14 @@ def tile_denseattentiononehead_pb_kernel(tc, q, h_rot, out):
 
         def tr(x, b, rt):
             transpose_rows(x, b, rt, nc.scalar.copy)
+
+        def trv(x, b, rt):
+            transpose_rows(x, b, rt, nc.vector.tensor_copy)
+
+        def warm(n):
+            bank = psum.tile([P, 512], F32, name="bank", tag="bank")
+            for i in range(n):
+                nc.tensor.matmul(bank[:], lhsT=blank[:, 0:P], rhs=blank[:], start=True, stop=True)
 
         def qz(x, b, rt):
             quantise(("t", x, b, rt), 256)
@@ -219,103 +227,106 @@ def tile_denseattentiononehead_pb_kernel(tc, q, h_rot, out):
                 drain(b, it, nh, bank, nc.vector.tensor_copy)
             pending.clear()
 
-        def step(s):
-            if s < STEPS:
-                scores(s, range(2))
-            if s >= LEAD:
-                outputs(s - LEAD)
+        def sc(s):
+            scores(s, range(2))
 
         for rt in range(4):
             tr("h", 0, rt)
-        tr("q", 0, 0)
+        kv(0, 0, 0)
         for rt in range(4):
             qz("h", 0, rt)
-        qz("q", 0, 0)
-        tr("h", 0, 4)
-        tr("h", 0, 5)
-        kv(0, 0, 0)
-        scores(0, range(1))
-        for rt in range(6, 8):
+        for rt in range(4, 8):
             tr("h", 0, rt)
-        tr("q", 0, 1)
+        kq(0, 0, 0)
         for rt in range(4, 8):
             qz("h", 0, rt)
-        qz("q", 0, 1)
-        scores(0, range(1, 2))
-        kq(0, 0, 0)
-        tr("q", 0, 2)
-        tr("q", 0, 3)
-        qz("q", 0, 2)
-        qz("q", 0, 3)
-        step(1)
+        for rt in range(4):
+            tr("q", 0, rt)
+        for rt in range(4):
+            qz("q", 0, rt)
+        warm(2)
+        for rt in range(4, 4 + 2):
+            tr("q", 0, rt)
+        sc(0)
+        sc(1)
         kv(0, 0, 1)
         qs(0)
-        kq(0, 0, 1)
-        step(2)
-        kv(0, 1, 0)
-        for rt in range(4, 8):
+        sc(2)
+        for rt in range(4 + 2, 8):
             tr("q", 0, rt)
-        qs(1)
-        kq(0, 1, 0)
-        step(3)
+        for rt in range(4):
+            tr("h", 1, rt)
+        kv(0, 1, 0)
+        kq(0, 0, 1)
         for rt in range(4, 8):
             qz("q", 0, rt)
+        qs(1)
+        sc(3)
+        sc(4)
+        kq(0, 1, 0)
         kv(0, 1, 1)
         qs(2)
+        for rt in range(4, 8):
+            tr("h", 1, rt)
         kq(0, 1, 1)
-        for rt in range(4):
-            tr("h", 1, rt)
-        step(4)
         qs(3)
+        sc(5)
+        outputs(0)
+        for rt in range(4):
+            tr("q", 1, rt)
+        qs(4)
         for rt in range(4):
             qz("h", 1, rt)
-        for rt in range(4, 8):
-            tr("h", 1, rt)
-        step(5)
-        load_blocks(1, 1)
-        qs(4)
-        turn_blocks(1, 0, 0)
-        turn_blocks(1, 0, 1)
-        step(6)
+        sc(6)
+        outputs(1)
         qs(5)
-        quantise_blocks(1, 0, 0)
-        quantise_blocks(1, 0, 1)
         for rt in range(4, 8):
             qz("h", 1, rt)
-        step(7)
+        for rt in range(4):
+            qz("q", 1, rt)
+        sc(7)
+        outputs(2, (1,))
         qs(6)
         kv(1, 0, 0)
-        step(8)
+        flush()
+        sc(8)
+        outputs(3)
         qs(7)
         kq(1, 0, 0)
         kv(1, 1, 0)
-        flush()
-        step(9)
+        sc(9)
+        outputs(4)
         qs(8)
         kq(1, 1, 0)
         turn_blocks(1, 1, 0)
-        flush()
-        step(10)
+        sc(10)
+        outputs(5)
         qs(9)
         turn_blocks(1, 1, 1)
         quantise_blocks(1, 1, 0)
         quantise_blocks(1, 1, 1)
-        flush()
-        step(11)
+        sc(11)
+        outputs(6, (1,))
         qs(10)
         kv(1, 0, 1)
         flush()
-        step(12)
+        sc(12)
+        outputs(7, (1,))
         qs(11)
         kq(1, 0, 1)
         kv(1, 1, 1)
         flush()
-        step(13)
-        qs(12)
-        kq(1, 1, 1)
-        flush()
-        for s in range(14, STEPS + LEAD):
-            step(s)
-            if s - 1 < STEPS:
-                qs(s - 1)
+        for s in range(13, 16):
+            sc(s)
+            for i in range(2 * s - 18, min(2 * s - 16, 13)):
+                if i % 2 == 0:
+                    qs(s - 1)
+                if i == 8:
+                    kq(1, 1, 1)
+                outputs(i, (1,))
+                flush()
+        for s in range(13, 16):
+            outputs(s, (1,))
+            if s == 13:
+                qs(15)
             flush()

@@ -31,8 +31,6 @@ def tile_denseattentiononehead_pb_kernel(tc, q, h_rot, out):
         psum = ctx.enter_context(tc.psum_pool(name="psum", bufs=8))
         ctx.enter_context(tc.manual_schedule())
 
-        blank = const.tile([P, 512], BF16, name="blank", align_bytes=64)
-        nc.gpsimd.memset(blank[:], 0.0)
         ident = const.tile([P, P], F32, name="ident")
         make_identity(nc, ident[:])
 
@@ -211,11 +209,6 @@ def tile_denseattentiononehead_pb_kernel(tc, q, h_rot, out):
         def trv(x, b, rt):
             transpose_rows(x, b, rt, nc.vector.tensor_copy)
 
-        def warm(n):
-            bank = psum.tile([P, 512], F32, name="bank", tag="bank")
-            for i in range(n):
-                nc.tensor.matmul(bank[:], lhsT=blank[:, 0:P], rhs=blank[:], start=True, stop=True)
-
         def qz(x, b, rt):
             quantise(("t", x, b, rt), 256)
 
@@ -237,96 +230,105 @@ def tile_denseattentiononehead_pb_kernel(tc, q, h_rot, out):
             qz("h", 0, rt)
         for rt in range(4, 8):
             tr("h", 0, rt)
-        kq(0, 0, 0)
+        for rt in range(4):
+            tr("q", 0, rt)
         for rt in range(4, 8):
             qz("h", 0, rt)
         for rt in range(4):
-            tr("q", 0, rt)
-        for rt in range(4):
             qz("q", 0, rt)
-        warm(2)
-        for rt in range(4, 4 + 2):
-            tr("q", 0, rt)
         sc(0)
-        sc(1)
-        kv(0, 0, 1)
-        qs(0)
-        sc(2)
-        for rt in range(4 + 2, 8):
-            tr("q", 0, rt)
-        for rt in range(4):
-            tr("h", 1, rt)
+        kq(0, 0, 0)
         kv(0, 1, 0)
-        kq(0, 0, 1)
+        sc(1)
+        qs(0)
+        kq(0, 1, 0)
+        sc(2)
+        kv(0, 0, 1)
+        qs(1)
+        tr("q", 0, 4)
+        tr("q", 0, 5)
+        tr("q", 0, 6)
+        tr("q", 0, 7)
+        tr("h", 1, 0)
+        tr("h", 1, 1)
+        tr("h", 1, 2)
+        tr("h", 1, 3)
+        sc(3)
         for rt in range(4, 8):
             qz("q", 0, rt)
-        qs(1)
-        sc(3)
-        sc(4)
-        kq(0, 1, 0)
-        kv(0, 1, 1)
+        kq(0, 0, 1)
         qs(2)
-        for rt in range(4, 8):
-            tr("h", 1, rt)
-        kq(0, 1, 1)
+        sc(4)
+        for rt in range(4):
+            qz("h", 1, rt)
+        kv(0, 1, 1)
         qs(3)
         sc(5)
-        outputs(0)
-        for rt in range(4):
-            tr("q", 1, rt)
+        kq(0, 1, 1)
         qs(4)
-        for rt in range(4):
-            qz("h", 1, rt)
+        tr("h", 1, 4)
+        trv("h", 1, 5)
+        tr("h", 1, 6)
+        trv("h", 1, 7)
+        tr("q", 1, 0)
+        trv("q", 1, 1)
+        tr("q", 1, 2)
+        trv("q", 1, 3)
         sc(6)
-        outputs(1)
-        qs(5)
+        outputs(0)
         for rt in range(4, 8):
             qz("h", 1, rt)
+        qs(5)
         for rt in range(4):
             qz("q", 1, rt)
         sc(7)
-        outputs(2, (1,))
+        outputs(1)
         qs(6)
         kv(1, 0, 0)
-        flush()
         sc(8)
-        outputs(3)
-        qs(7)
+        outputs(2)
         kq(1, 0, 0)
+        qs(7)
         kv(1, 1, 0)
         sc(9)
-        outputs(4)
-        qs(8)
-        kq(1, 1, 0)
+        outputs(3)
         turn_blocks(1, 1, 0)
-        sc(10)
-        outputs(5)
-        qs(9)
+        kq(1, 1, 0)
+        qs(8)
         turn_blocks(1, 1, 1)
+        sc(10)
+        outputs(4)
         quantise_blocks(1, 1, 0)
+        qs(9)
         quantise_blocks(1, 1, 1)
-        sc(11)
-        outputs(6, (1,))
-        qs(10)
         kv(1, 0, 1)
-        flush()
-        sc(12)
-        outputs(7, (1,))
-        qs(11)
+        sc(11)
+        outputs(5)
+        outputs(6)
+        qs(10)
         kq(1, 0, 1)
+        sc(12)
+        outputs(7)
+        qs(11)
         kv(1, 1, 1)
+        sc(13)
+        kq(1, 1, 1)
+        qs(12)
+        outputs(8, (1,))
         flush()
-        for s in range(13, 16):
-            sc(s)
-            for i in range(2 * s - 18, min(2 * s - 16, 13)):
-                if i % 2 == 0:
-                    qs(s - 1)
-                if i == 8:
-                    kq(1, 1, 1)
-                outputs(i, (1,))
-                flush()
+        outputs(9, (1,))
+        flush()
+        sc(14)
+        outputs(10, (1,))
+        flush()
+        outputs(11, (1,))
+        flush()
+        qs(13)
+        sc(15)
+        outputs(12, (1,))
+        flush()
+        qs(14)
+        qs(15)
         for s in range(13, 16):
             outputs(s, (1,))
-            if s == 13:
-                qs(15)
             flush()

@@ -80,38 +80,47 @@ def tile_denseattentiononehead_pb_kernel(tc, q, h_rot, out):
             for t in range(4):
                 transpose_rows(x, b, 4 * half + t, nc.vector.tensor_copy if (share and t == 0) else nc.scalar.copy)
 
-        def load_blocks(b, half):
-            blocks[half] = inputs.tile([P, 4 * H], BF16, name="blk_q%d%d" % (b, half), align_bytes=64)
+        def load_blocks(first, tiles):
+            groups = 8 * tiles
+            blocks[first] = inputs.tile([P, 128 * groups], BF16, name="blk_%d" % first, align_bytes=64)
             for g in range(2):
                 for qu in range(4):
                     for u in range(2):
                         k0 = 512 * g + 256 * u + 64 * qu
+                        cols = slice(64 * groups * g, 64 * groups * (g + 1))
                         nc.sync.dma_start(
-                            out=blocks[half][32 * qu + u : 32 * (qu + 1) : 2, 2048 * g : 2048 * (g + 1)].rearrange(
-                                "c (r w) -> c r w", w=64
-                            ),
-                            in_=q[b, 512 * half : 512 * (half + 1), k0 : k0 + 64].rearrange("(r c) w -> c r w", c=16),
+                            out=blocks[first][32 * qu + u : 32 * (qu + 1) : 2, cols].rearrange("c (r w) -> c r w", w=64),
+                            in_=q[1, P * first : P * (first + tiles), k0 : k0 + 64].rearrange("(r c) w -> c r w", c=16),
                         )
 
-        def turn_blocks(b, half, g):
-            turned = stage_q.tile([P, 2048], BF16, name="g_q", tag="g_q", align_bytes=64)
+        def turn_blocks(first, tiles, g):
+            width = 512 * tiles
+            turned = stage_q.tile([P, width], BF16, name="g_q%d" % tiles, tag="g_q%d" % tiles, align_bytes=64)
             nc.vector.transpose(
-                out=turned[:].bitcast(F32), in_=blocks[half][:, 2048 * g : 2048 * (g + 1)].bitcast(F32)
+                out=turned[:].bitcast(F32), in_=blocks[first][:, width * g : width * (g + 1)].bitcast(F32)
             )
-            staged[("b", half, g)] = turned
+            staged[("b", first, g)] = turned
 
-        def quantise_blocks(b, half, g):
+        def quantise_blocks(first, tiles, g):
+            width = P * tiles
             if g == 0:
-                block_words[half] = codes.tile([P, 1024], U32, name="c_b%d" % half, align_bytes=64)
-                block_scales[half] = codes.tile([P, 1024], U8, name="s_b%d" % half, align_bytes=64)
-            cols = slice(512 * g, 512 * (g + 1))
+                block_words[first] = codes.tile([P, 2 * width], U32, name="c_b%d" % first, align_bytes=64)
+                block_scales[first] = codes.tile([P, 2 * width], U8, name="s_b%d" % first, align_bytes=64)
+            cols = slice(width * g, width * (g + 1))
             nc.vector.quantize_mx(
-                out=block_words[half][:, cols].bitcast(FP8X4),
-                scales=block_scales[half][:, cols],
-                in_=staged[("b", half, g)][:],
+                out=block_words[first][:, cols].bitcast(FP8X4),
+                scales=block_scales[first][:, cols],
+                in_=staged[("b", first, g)][:],
             )
-            for t in range(4):
-                mx[("t", "q", b, 4 * half + t)] = (block_words[half], block_scales[half], (P * t, 512 + P * t))
+            for t in range(tiles):
+                mx[("t", "q", 1, first + t)] = (block_words[first], block_scales[first], (P * t, width + P * t))
+
+        def load_plain(tiles):
+            rows[("q", 1, 0)] = inputs.tile([P, tiles * H], BF16, name="in_q1", align_bytes=64)
+            nc.sync.dma_start(
+                out=rows[("q", 1, 0)][:].rearrange("p (t w) -> p t w", t=tiles),
+                in_=q[1, 0 : P * tiles, :].rearrange("(t p) w -> p t w", p=P),
+            )
 
         def quantise_rows(x, b, half):
             for t in range(4):
@@ -183,7 +192,7 @@ def tile_denseattentiononehead_pb_kernel(tc, q, h_rot, out):
             result = stage_o.tile([P, 512], F32, name="o_sb", tag="o_sb")
             engine(out=result[:], in_=bank[:])
             cols = slice(512 * nh, 512 * (nh + 1))
-            if b == 0 or it < 4:
+            if b == 0:
                 nc.sync.dma_start(out=out_view[b, it // 4, it % 4, :, cols], in_=result[:])
             else:
                 nc.sync.dma_start(out=out[b, P * it : P * (it + 1), cols], in_=result[:])
@@ -194,8 +203,9 @@ def tile_denseattentiononehead_pb_kernel(tc, q, h_rot, out):
         load("q", 0, 1, range(4))
         load("h", 1, 0, None)
         load("h", 1, 1, None)
-        load("q", 1, 0, None)
-        load_blocks(1, 1)
+        load_plain(2)
+        load_blocks(2, 2)
+        load_blocks(4, 4)
 
         def kv(b, g2, nh):
             values(b, g2, nh)
@@ -272,14 +282,12 @@ def tile_denseattentiononehead_pb_kernel(tc, q, h_rot, out):
         trv("h", 1, 7)
         tr("q", 1, 0)
         trv("q", 1, 1)
-        tr("q", 1, 2)
-        trv("q", 1, 3)
         sc(6)
         outputs(0)
         for rt in range(4, 8):
             qz("h", 1, rt)
         qs(5)
-        for rt in range(4):
+        for rt in range(2):
             qz("q", 1, rt)
         sc(7)
         outputs(1)
@@ -287,30 +295,34 @@ def tile_denseattentiononehead_pb_kernel(tc, q, h_rot, out):
         kv(1, 0, 0)
         sc(8)
         outputs(2)
+        turn_blocks(2, 2, 0)
         kq(1, 0, 0)
+        turn_blocks(2, 2, 1)
         qs(7)
-        kv(1, 1, 0)
+        quantise_blocks(2, 2, 0)
+        quantise_blocks(2, 2, 1)
         sc(9)
         outputs(3)
-        turn_blocks(1, 1, 0)
-        kq(1, 1, 0)
+        kv(1, 1, 0)
         qs(8)
-        turn_blocks(1, 1, 1)
+        kq(1, 1, 0)
         sc(10)
         outputs(4)
-        quantise_blocks(1, 1, 0)
+        turn_blocks(4, 4, 0)
         qs(9)
-        quantise_blocks(1, 1, 1)
-        kv(1, 0, 1)
+        turn_blocks(4, 4, 1)
+        quantise_blocks(4, 4, 0)
         sc(11)
         outputs(5)
         outputs(6)
+        quantise_blocks(4, 4, 1)
+        kv(1, 0, 1)
         qs(10)
-        kq(1, 0, 1)
         sc(12)
         outputs(7)
-        qs(11)
+        kq(1, 0, 1)
         kv(1, 1, 1)
+        qs(11)
         sc(13)
         kq(1, 1, 1)
         qs(12)

@@ -106,12 +106,14 @@ def tile_denseattentiononehead_pb_kernel(tc, q, h_rot, out):
             if g == 0:
                 block_words[first] = codes.tile([P, 2 * width], U32, name="c_b%d" % first, align_bytes=64)
                 block_scales[first] = codes.tile([P, 2 * width], U8, name="s_b%d" % first, align_bytes=64)
-            cols = slice(width * g, width * (g + 1))
-            nc.vector.quantize_mx(
-                out=block_words[first][:, cols].bitcast(FP8X4),
-                scales=block_scales[first][:, cols],
-                in_=staged[("b", first, g)][:],
-            )
+            for t in range(0, tiles, 2):
+                last = min(t + 2, tiles)
+                cols = slice(width * g + P * t, width * g + P * last)
+                nc.vector.quantize_mx(
+                    out=block_words[first][:, cols].bitcast(FP8X4),
+                    scales=block_scales[first][:, cols],
+                    in_=staged[("b", first, g)][:, 512 * t : 512 * last],
+                )
             for t in range(tiles):
                 mx[("t", "q", 1, first + t)] = (block_words[first], block_scales[first], (P * t, width + P * t))
 
@@ -198,13 +200,14 @@ def tile_denseattentiononehead_pb_kernel(tc, q, h_rot, out):
                 nc.sync.dma_start(out=out[b, P * it : P * (it + 1), cols], in_=result[:])
 
         load("h", 0, 0, range(4))
+        load("q", 0, 0, range(1))
         load("h", 0, 1, range(4))
-        load("q", 0, 0, range(4))
-        load("q", 0, 1, range(4))
+        load("q", 0, 0, range(1, 4))
+        load("q", 0, 1, None)
         load("h", 1, 0, None)
         load("h", 1, 1, None)
-        load_plain(2)
-        load_blocks(2, 2)
+        load_plain(1)
+        load_blocks(1, 3)
         load_blocks(4, 4)
 
         def kv(b, g2, nh):
@@ -233,23 +236,32 @@ def tile_denseattentiononehead_pb_kernel(tc, q, h_rot, out):
         def sc(s):
             scores(s, range(2))
 
-        for rt in range(4):
-            tr("h", 0, rt)
+        tr("h", 0, 0)
+        tr("h", 0, 1)
+        tr("h", 0, 2)
+        tr("h", 0, 3)
         kv(0, 0, 0)
         for rt in range(4):
             qz("h", 0, rt)
-        for rt in range(4, 8):
-            tr("h", 0, rt)
-        for rt in range(4):
-            tr("q", 0, rt)
+        tr("q", 0, 0)
+        for rt in range(1):
+            qz("q", 0, rt)
+        tr("h", 0, 4)
+        tr("h", 0, 5)
+        tr("h", 0, 6)
+        tr("h", 0, 7)
+        scores(0, range(1))
+        tr("q", 0, 1)
+        tr("q", 0, 2)
+        tr("q", 0, 3)
         for rt in range(4, 8):
             qz("h", 0, rt)
-        for rt in range(4):
+        for rt in range(1, 4):
             qz("q", 0, rt)
-        sc(0)
+        scores(0, range(1, 2))
+        sc(1)
         kq(0, 0, 0)
         kv(0, 1, 0)
-        sc(1)
         qs(0)
         kq(0, 1, 0)
         sc(2)
@@ -281,26 +293,25 @@ def tile_denseattentiononehead_pb_kernel(tc, q, h_rot, out):
         tr("h", 1, 6)
         trv("h", 1, 7)
         tr("q", 1, 0)
-        trv("q", 1, 1)
         sc(6)
         outputs(0)
         for rt in range(4, 8):
             qz("h", 1, rt)
         qs(5)
-        for rt in range(2):
+        for rt in range(1):
             qz("q", 1, rt)
         sc(7)
         outputs(1)
+        turn_blocks(1, 3, 0)
         qs(6)
+        turn_blocks(1, 3, 1)
+        quantise_blocks(1, 3, 0)
+        quantise_blocks(1, 3, 1)
         kv(1, 0, 0)
         sc(8)
         outputs(2)
-        turn_blocks(2, 2, 0)
         kq(1, 0, 0)
-        turn_blocks(2, 2, 1)
         qs(7)
-        quantise_blocks(2, 2, 0)
-        quantise_blocks(2, 2, 1)
         sc(9)
         outputs(3)
         kv(1, 1, 0)
@@ -308,19 +319,19 @@ def tile_denseattentiononehead_pb_kernel(tc, q, h_rot, out):
         kq(1, 1, 0)
         sc(10)
         outputs(4)
-        turn_blocks(4, 4, 0)
+        outputs(5)
+        kv(1, 0, 1)
         qs(9)
+        sc(11)
+        outputs(6)
+        outputs(7)
+        turn_blocks(4, 4, 0)
+        kq(1, 0, 1)
+        qs(10)
         turn_blocks(4, 4, 1)
         quantise_blocks(4, 4, 0)
-        sc(11)
-        outputs(5)
-        outputs(6)
         quantise_blocks(4, 4, 1)
-        kv(1, 0, 1)
-        qs(10)
         sc(12)
-        outputs(7)
-        kq(1, 0, 1)
         kv(1, 1, 1)
         qs(11)
         sc(13)

@@ -23,11 +23,12 @@ def tile_denseattentiononehead_pb_kernel(tc, q, h_rot, out):
         const = ctx.enter_context(tc.tile_pool(name="const", bufs=1))
         inputs = ctx.enter_context(tc.tile_pool(name="inputs", bufs=1))
         codes = ctx.enter_context(tc.tile_pool(name="codes", bufs=1))
-        stage_t = ctx.enter_context(tc.tile_pool(name="stage_t", bufs=12))
+        stage_t = ctx.enter_context(tc.tile_pool(name="stage_t", bufs=8))
         stage_q = ctx.enter_context(tc.tile_pool(name="stage_q", bufs=2))
         stage_h = ctx.enter_context(tc.tile_pool(name="stage_h", bufs=3))
         stage_s = ctx.enter_context(tc.tile_pool(name="stage_s", bufs=4))
-        stage_o = ctx.enter_context(tc.tile_pool(name="stage_o", bufs=16))
+        stage_w = ctx.enter_context(tc.tile_pool(name="stage_w", bufs=6))
+        stage_o = ctx.enter_context(tc.tile_pool(name="stage_o", bufs=10))
         psum = ctx.enter_context(tc.psum_pool(name="psum", bufs=8))
         ctx.enter_context(tc.manual_schedule())
 
@@ -42,6 +43,7 @@ def tile_denseattentiononehead_pb_kernel(tc, q, h_rot, out):
         rows = {}
         blocks = {}
         pending = []
+        wide = {}
         block_words = {}
         block_scales = {}
         staged = {}
@@ -56,6 +58,14 @@ def tile_denseattentiononehead_pb_kernel(tc, q, h_rot, out):
             else:
                 for t in pieces:
                     nc.sync.dma_start(out=dst[:, t * H : (t + 1) * H], in_=dram[x][b, half, :, t, :])
+
+        def load2(x, b, half, t):
+            if (x, b, half) not in rows:
+                rows[(x, b, half)] = inputs.tile([P, 4 * H], BF16, name="in_%s%d%d" % (x, b, half), align_bytes=64)
+            nc.sync.dma_start(
+                out=rows[(x, b, half)][:, t * H : (t + 2) * H].rearrange("p (t w) -> p t w", t=2),
+                in_=dram[x][b, half, :, t : t + 2, :],
+            )
 
         def quantise(key, width):
             words = codes.tile([P, width], U32, name="c_%s_%s_%d_%d" % key, align_bytes=64)
@@ -106,14 +116,12 @@ def tile_denseattentiononehead_pb_kernel(tc, q, h_rot, out):
             if g == 0:
                 block_words[first] = codes.tile([P, 2 * width], U32, name="c_b%d" % first, align_bytes=64)
                 block_scales[first] = codes.tile([P, 2 * width], U8, name="s_b%d" % first, align_bytes=64)
-            for t in range(0, tiles, 2):
-                last = min(t + 2, tiles)
-                cols = slice(width * g + P * t, width * g + P * last)
-                nc.vector.quantize_mx(
-                    out=block_words[first][:, cols].bitcast(FP8X4),
-                    scales=block_scales[first][:, cols],
-                    in_=staged[("b", first, g)][:, 512 * t : 512 * last],
-                )
+            cols = slice(width * g, width * (g + 1))
+            nc.vector.quantize_mx(
+                out=block_words[first][:, cols].bitcast(FP8X4),
+                scales=block_scales[first][:, cols],
+                in_=staged[("b", first, g)][:],
+            )
             for t in range(tiles):
                 mx[("t", "q", 1, first + t)] = (block_words[first], block_scales[first], (P * t, width + P * t))
 
@@ -191,24 +199,30 @@ def tile_denseattentiononehead_pb_kernel(tc, q, h_rot, out):
                     drain(b, it, nh, bank, nc.scalar.copy)
 
         def drain(b, it, nh, bank, engine):
-            result = stage_o.tile([P, 512], F32, name="o_sb", tag="o_sb")
-            engine(out=result[:], in_=bank[:])
             cols = slice(512 * nh, 512 * (nh + 1))
-            if b == 0:
-                nc.sync.dma_start(out=out_view[b, it // 4, it % 4, :, cols], in_=result[:])
+            if b == 0 or it < 2:
+                if nh == 0:
+                    wide[(b, it)] = stage_w.tile([P, H], F32, name="w_sb", tag="w_sb")
+                engine(out=wide[(b, it)][:, cols], in_=bank[:])
+                if nh == 1:
+                    nc.sync.dma_start(out=out_view[b, it // 4, it % 4] if b == 0 else out[b, P * it : P * (it + 1), :], in_=wide[(b, it)][:])
             else:
+                result = stage_o.tile([P, 512], F32, name="o_sb", tag="o_sb")
+                engine(out=result[:], in_=bank[:])
                 nc.sync.dma_start(out=out[b, P * it : P * (it + 1), cols], in_=result[:])
 
-        load("h", 0, 0, range(4))
+        load("h", 0, 0, range(2))
+        load2("h", 0, 0, 2)
         load("q", 0, 0, range(1))
-        load("h", 0, 1, range(4))
-        load("q", 0, 0, range(1, 4))
+        load2("h", 0, 1, 0)
+        load2("h", 0, 1, 2)
+        load("q", 0, 0, range(1, 2))
+        load2("q", 0, 0, 2)
         load("q", 0, 1, None)
         load("h", 1, 0, None)
         load("h", 1, 1, None)
-        load_plain(1)
-        load_blocks(1, 3)
-        load_blocks(4, 4)
+        for first in range(0, 8, 2):
+            load_blocks(first, 2)
 
         def kv(b, g2, nh):
             values(b, g2, nh)
@@ -292,21 +306,18 @@ def tile_denseattentiononehead_pb_kernel(tc, q, h_rot, out):
         trv("h", 1, 5)
         tr("h", 1, 6)
         trv("h", 1, 7)
-        tr("q", 1, 0)
         sc(6)
         outputs(0)
         for rt in range(4, 8):
             qz("h", 1, rt)
         qs(5)
-        for rt in range(1):
-            qz("q", 1, rt)
         sc(7)
         outputs(1)
-        turn_blocks(1, 3, 0)
+        turn_blocks(0, 2, 0)
         qs(6)
-        turn_blocks(1, 3, 1)
-        quantise_blocks(1, 3, 0)
-        quantise_blocks(1, 3, 1)
+        turn_blocks(0, 2, 1)
+        quantise_blocks(0, 2, 0)
+        quantise_blocks(0, 2, 1)
         kv(1, 0, 0)
         sc(8)
         outputs(2)
@@ -314,29 +325,37 @@ def tile_denseattentiononehead_pb_kernel(tc, q, h_rot, out):
         qs(7)
         sc(9)
         outputs(3)
-        kv(1, 1, 0)
+        turn_blocks(2, 2, 0)
         qs(8)
-        kq(1, 1, 0)
+        turn_blocks(2, 2, 1)
+        quantise_blocks(2, 2, 0)
+        quantise_blocks(2, 2, 1)
+        kv(1, 1, 0)
         sc(10)
         outputs(4)
         outputs(5)
+        kq(1, 1, 0)
         kv(1, 0, 1)
         qs(9)
         sc(11)
         outputs(6)
         outputs(7)
-        turn_blocks(4, 4, 0)
+        turn_blocks(4, 2, 0)
         kq(1, 0, 1)
         qs(10)
-        turn_blocks(4, 4, 1)
-        quantise_blocks(4, 4, 0)
-        quantise_blocks(4, 4, 1)
+        turn_blocks(4, 2, 1)
+        quantise_blocks(4, 2, 0)
+        quantise_blocks(4, 2, 1)
         sc(12)
         kv(1, 1, 1)
         qs(11)
-        sc(13)
+        turn_blocks(6, 2, 0)
         kq(1, 1, 1)
+        turn_blocks(6, 2, 1)
+        sc(13)
         qs(12)
+        quantise_blocks(6, 2, 0)
+        quantise_blocks(6, 2, 1)
         outputs(8, (1,))
         flush()
         outputs(9, (1,))
@@ -344,14 +363,17 @@ def tile_denseattentiononehead_pb_kernel(tc, q, h_rot, out):
         sc(14)
         outputs(10, (1,))
         flush()
+        qs(13)
         outputs(11, (1,))
         flush()
-        qs(13)
         sc(15)
+        qs(14)
         outputs(12, (1,))
         flush()
-        qs(14)
         qs(15)
-        for s in range(13, 16):
-            outputs(s, (1,))
-            flush()
+        outputs(13, (1,))
+        flush()
+        outputs(14, (1,))
+        flush()
+        outputs(15, (1,))
+        flush()

from contextlib import ExitStack

import concourse.mybir as mybir
from concourse.masks import make_identity

F32 = mybir.dt.float32
BF16 = mybir.dt.bfloat16
U32 = mybir.dt.uint32
U8 = mybir.dt.uint8
FP8X4 = mybir.dt.float8_e4m3fn_x4

L = 1024
H = 1024
P = 128
FLOPS = 8 * L * L * H

STEPS = 16


def tile_denseattentiononehead_pb_kernel(tc, q, h_rot, out):
    nc = tc.nc
    with ExitStack() as ctx:
        const = ctx.enter_context(tc.tile_pool(name="const", bufs=1))
        inputs = ctx.enter_context(tc.tile_pool(name="inputs", bufs=1))
        codes = ctx.enter_context(tc.tile_pool(name="codes", bufs=1))
        stage_t = ctx.enter_context(tc.tile_pool(name="stage_t", bufs=8))
        stage_q = ctx.enter_context(tc.tile_pool(name="stage_q", bufs=2))
        stage_h = ctx.enter_context(tc.tile_pool(name="stage_h", bufs=3))
        stage_s = ctx.enter_context(tc.tile_pool(name="stage_s", bufs=4))
        stage_w = ctx.enter_context(tc.tile_pool(name="stage_w", bufs=6))
        stage_o = ctx.enter_context(tc.tile_pool(name="stage_o", bufs=10))
        psum = ctx.enter_context(tc.psum_pool(name="psum", bufs=8))
        ctx.enter_context(tc.manual_schedule())

        ident = const.tile([P, P], F32, name="ident")
        make_identity(nc, ident[:])

        dram = {
            "q": q.rearrange("b (a p t) w -> b a p t w", a=2, p=P, t=4),
            "h": h_rot.rearrange("b (a p t) w -> b a p t w", a=2, p=P, t=4),
        }
        out_view = out.rearrange("b (a p t) n -> b a t p n", a=2, p=P, t=4)
        rows = {}
        blocks = {}
        pending = []
        wide = {}
        block_words = {}
        block_scales = {}
        staged = {}
        mx = {}

        def load(x, b, half, pieces):
            if (x, b, half) not in rows:
                rows[(x, b, half)] = inputs.tile([P, 4 * H], BF16, name="in_%s%d%d" % (x, b, half), align_bytes=64)
            dst = rows[(x, b, half)]
            if pieces is None:
                nc.sync.dma_start(out=dst[:].rearrange("p (t w) -> p t w", t=4), in_=dram[x][b, half])
            else:
                for t in pieces:
                    nc.sync.dma_start(out=dst[:, t * H : (t + 1) * H], in_=dram[x][b, half, :, t, :])

        def load2(x, b, half, t):
            if (x, b, half) not in rows:
                rows[(x, b, half)] = inputs.tile([P, 4 * H], BF16, name="in_%s%d%d" % (x, b, half), align_bytes=64)
            nc.sync.dma_start(
                out=rows[(x, b, half)][:, t * H : (t + 2) * H].rearrange("p (t w) -> p t w", t=2),
                in_=dram[x][b, half, :, t : t + 2, :],
            )

        def quantise(key, width):
            words = codes.tile([P, width], U32, name="c_%s_%s_%d_%d" % key, align_bytes=64)
            scales = codes.tile([P, width], U8, name="s_%s_%s_%d_%d" % key, align_bytes=64)
            nc.vector.quantize_mx(out=words[:].bitcast(FP8X4), scales=scales[:], in_=staged[key][:])
            mx[key] = (words, scales, (0, P))

        def transpose_rows(x, b, rt, engine):
            words = rows[(x, b, rt // 4)][:].bitcast(F32)
            bank = psum.tile([P, 512], F32, name="bank", tag="bank")
            for wt in range(4):
                col = 512 * (rt % 4) + P * wt
                nc.tensor.transpose(bank[:, P * wt : P * (wt + 1)], words[:, col : col + P], ident[:])
            grouped = stage_t.tile([P, 1024], BF16, name="g_t", tag="g_t", align_bytes=64)
            engine(
                out=grouped[:].bitcast(F32).rearrange("p (g r u) -> p g r u", g=2, r=P, u=2),
                in_=bank[:].rearrange("p (g u r) -> p g r u", g=2, u=2, r=P),
            )
            staged[("t", x, b, rt)] = grouped

        def transposes(x, b, half, share):
            for t in range(4):
                transpose_rows(x, b, 4 * half + t, nc.vector.tensor_copy if (share and t == 0) else nc.scalar.copy)

        def load_blocks(first, tiles):
            groups = 8 * tiles
            blocks[first] = inputs.tile([P, 128 * groups], BF16, name="blk_%d" % first, align_bytes=64)
            for g in range(2):
                for qu in range(4):
                    for u in range(2):
                        k0 = 512 * g + 256 * u + 64 * qu
                        cols = slice(64 * groups * g, 64 * groups * (g + 1))
                        nc.sync.dma_start(
                            out=blocks[first][32 * qu + u : 32 * (qu + 1) : 2, cols].rearrange("c (r w) -> c r w", w=64),
                            in_=q[1, P * first : P * (first + tiles), k0 : k0 + 64].rearrange("(r c) w -> c r w", c=16),
                        )

        def turn_blocks(first, tiles, g):
            width = 512 * tiles
            turned = stage_q.tile([P, width], BF16, name="g_q%d" % tiles, tag="g_q%d" % tiles, align_bytes=64)
            nc.vector.transpose(
                out=turned[:].bitcast(F32), in_=blocks[first][:, width * g : width * (g + 1)].bitcast(F32)
            )
            staged[("b", first, g)] = turned

        def quantise_blocks(first, tiles, g):
            width = P * tiles
            if g == 0:
                block_words[first] = codes.tile([P, 2 * width], U32, name="c_b%d" % first, align_bytes=64)
                block_scales[first] = codes.tile([P, 2 * width], U8, name="s_b%d" % first, align_bytes=64)
            cols = slice(width * g, width * (g + 1))
            nc.vector.quantize_mx(
                out=block_words[first][:, cols].bitcast(FP8X4),
                scales=block_scales[first][:, cols],
                in_=staged[("b", first, g)][:],
            )
            for t in range(tiles):
                mx[("t", "q", 1, first + t)] = (block_words[first], block_scales[first], (P * t, width + P * t))

        def load_plain(tiles):
            rows[("q", 1, 0)] = inputs.tile([P, tiles * H], BF16, name="in_q1", align_bytes=64)
            nc.sync.dma_start(
                out=rows[("q", 1, 0)][:].rearrange("p (t w) -> p t w", t=tiles),
                in_=q[1, 0 : P * tiles, :].rearrange("(t p) w -> p t w", p=P),
            )

        def quantise_rows(x, b, half):
            for t in range(4):
                quantise(("t", x, b, 4 * half + t), 256)

        def prepare(x, b, half, share):
            transposes(x, b, half, share)
            quantise_rows(x, b, half)

        def values(b, g2, nh):
            src = rows[("h", b, g2)][:].rearrange("p (t n) -> p t n", t=4)[:, :, 512 * nh : 512 * (nh + 1)]
            grouped = stage_h.tile([P, 2048], BF16, name="g_h", tag="g_h", align_bytes=64)
            nc.vector.tensor_copy(
                out=grouped[:].rearrange("p (c i t) -> p c t i", c=P, i=4, t=4),
                in_=src.rearrange("p t (c i) -> p c t i", i=4),
            )
            staged[("k", "h", 2 * b + g2, nh)] = grouped

        def scores(s, parts):
            b, it = divmod(s, 8)
            q_words, q_scales, q_cols = mx[("t", "q", b, it)]
            if 0 in parts:
                staged[("s", "s", b, it)] = stage_s.tile([P, 1024], BF16, name="g_s", tag="g_s", align_bytes=64)
            grouped = staged[("s", "s", b, it)]
            for g2 in parts:
                bank = psum.tile([P, 512], F32, name="bank", tag="bank")
                for t in range(4):
                    h_words, h_scales, h_cols = mx[("t", "h", b, 4 * g2 + t)]
                    for g in range(2):
                        hc = slice(h_cols[g], h_cols[g] + P)
                        qc = slice(q_cols[g], q_cols[g] + P)
                        nc.tensor.matmul_mx(
                            out=bank[:, P * t : P * (t + 1)],
                            lhsT=h_words[:, hc].bitcast(FP8X4),
                            lhsT_scale=h_scales[:, hc],
                            rhs=q_words[:, qc].bitcast(FP8X4),
                            rhs_scale=q_scales[:, qc],
                            start=(g == 0),
                            stop=(g == 1),
                        )
                nc.scalar.copy(
                    out=grouped[:, 512 * g2 : 512 * (g2 + 1)].rearrange("p (i t) -> p i t", t=4),
                    in_=bank[:].rearrange("p (t i) -> p i t", t=4),
                )

        def outputs(s, vec=()):
            b, it = divmod(s, 8)
            s_words, s_scales, s_cols = mx[("s", "s", b, it)]
            for nh in range(2):
                bank = psum.tile([P, 512], F32, name="bank", tag="bank")
                for g2 in range(2):
                    k_words, k_scales, k_cols = mx[("k", "h", 2 * b + g2, nh)]
                    cols = slice(P * g2, P * (g2 + 1))
                    nc.tensor.matmul_mx(
                        out=bank[:],
                        lhsT=s_words[:, cols].bitcast(FP8X4),
                        lhsT_scale=s_scales[:, cols],
                        rhs=k_words[:].bitcast(FP8X4),
                        rhs_scale=k_scales[:],
                        start=(g2 == 0),
                        stop=(g2 == 1),
                    )
                if nh in vec:
                    pending.append((b, it, nh, bank))
                else:
                    drain(b, it, nh, bank, nc.scalar.copy)

        def drain(b, it, nh, bank, engine):
            cols = slice(512 * nh, 512 * (nh + 1))
            if b == 0 or it < 2:
                if nh == 0:
                    wide[(b, it)] = stage_w.tile([P, H], F32, name="w_sb", tag="w_sb")
                engine(out=wide[(b, it)][:, cols], in_=bank[:])
                if nh == 1:
                    nc.sync.dma_start(out=out_view[b, it // 4, it % 4] if b == 0 else out[b, P * it : P * (it + 1), :], in_=wide[(b, it)][:])
            else:
                result = stage_o.tile([P, 512], F32, name="o_sb", tag="o_sb")
                engine(out=result[:], in_=bank[:])
                nc.sync.dma_start(out=out[b, P * it : P * (it + 1), cols], in_=result[:])

        load("h", 0, 0, range(2))
        load2("h", 0, 0, 2)
        load("q", 0, 0, range(1))
        load2("h", 0, 1, 0)
        load2("h", 0, 1, 2)
        load("q", 0, 0, range(1, 2))
        load2("q", 0, 0, 2)
        load("q", 0, 1, None)
        load("h", 1, 0, None)
        load("h", 1, 1, None)
        for first in range(0, 8, 2):
            load_blocks(first, 2)

        def kv(b, g2, nh):
            values(b, g2, nh)

        def kq(b, g2, nh):
            quantise(("k", "h", 2 * b + g2, nh), 512)

        def tr(x, b, rt):
            transpose_rows(x, b, rt, nc.scalar.copy)

        def trv(x, b, rt):
            transpose_rows(x, b, rt, nc.vector.tensor_copy)

        def qz(x, b, rt):
            quantise(("t", x, b, rt), 256)

        def qs(s):
            quantise(("s", "s", s // 8, s % 8), 256)

        def flush():
            for b, it, nh, bank in pending:
                drain(b, it, nh, bank, nc.vector.tensor_copy)
            pending.clear()

        def sc(s):
            scores(s, range(2))

        tr("h", 0, 0)
        tr("h", 0, 1)
        tr("h", 0, 2)
        tr("h", 0, 3)
        kv(0, 0, 0)
        for rt in range(4):
            qz("h", 0, rt)
        tr("q", 0, 0)
        for rt in range(1):
            qz("q", 0, rt)
        tr("h", 0, 4)
        tr("h", 0, 5)
        tr("h", 0, 6)
        tr("h", 0, 7)
        scores(0, range(1))
        tr("q", 0, 1)
        tr("q", 0, 2)
        tr("q", 0, 3)
        for rt in range(4, 8):
            qz("h", 0, rt)
        for rt in range(1, 4):
            qz("q", 0, rt)
        scores(0, range(1, 2))
        sc(1)
        kq(0, 0, 0)
        kv(0, 1, 0)
        qs(0)
        kq(0, 1, 0)
        sc(2)
        kv(0, 0, 1)
        qs(1)
        tr("q", 0, 4)
        tr("q", 0, 5)
        tr("q", 0, 6)
        tr("q", 0, 7)
        tr("h", 1, 0)
        tr("h", 1, 1)
        tr("h", 1, 2)
        tr("h", 1, 3)
        sc(3)
        for rt in range(4, 8):
            qz("q", 0, rt)
        kq(0, 0, 1)
        qs(2)
        sc(4)
        for rt in range(4):
            qz("h", 1, rt)
        kv(0, 1, 1)
        qs(3)
        sc(5)
        kq(0, 1, 1)
        qs(4)
        tr("h", 1, 4)
        trv("h", 1, 5)
        tr("h", 1, 6)
        trv("h", 1, 7)
        sc(6)
        outputs(0)
        for rt in range(4, 8):
            qz("h", 1, rt)
        qs(5)
        sc(7)
        outputs(1)
        turn_blocks(0, 2, 0)
        qs(6)
        turn_blocks(0, 2, 1)
        quantise_blocks(0, 2, 0)
        quantise_blocks(0, 2, 1)
        kv(1, 0, 0)
        sc(8)
        outputs(2)
        kq(1, 0, 0)
        qs(7)
        sc(9)
        outputs(3)
        turn_blocks(2, 2, 0)
        qs(8)
        turn_blocks(2, 2, 1)
        quantise_blocks(2, 2, 0)
        quantise_blocks(2, 2, 1)
        kv(1, 1, 0)
        sc(10)
        outputs(4)
        outputs(5)
        kq(1, 1, 0)
        kv(1, 0, 1)
        qs(9)
        sc(11)
        outputs(6)
        outputs(7)
        turn_blocks(4, 2, 0)
        kq(1, 0, 1)
        qs(10)
        turn_blocks(4, 2, 1)
        quantise_blocks(4, 2, 0)
        quantise_blocks(4, 2, 1)
        sc(12)
        kv(1, 1, 1)
        qs(11)
        turn_blocks(6, 2, 0)
        kq(1, 1, 1)
        turn_blocks(6, 2, 1)
        sc(13)
        qs(12)
        quantise_blocks(6, 2, 0)
        quantise_blocks(6, 2, 1)
        outputs(8, (1,))
        flush()
        outputs(9, (1,))
        flush()
        sc(14)
        outputs(10, (1,))
        flush()
        qs(13)
        outputs(11, (1,))
        flush()
        sc(15)
        qs(14)
        outputs(12, (1,))
        flush()
        qs(15)
        outputs(13, (1,))
        flush()
        outputs(14, (1,))
        flush()
        outputs(15, (1,))
        flush()
